import numpy as np
import ml_dtypes


def mxq(x, axis, fmt="e4m3"):
    dtype, down = {"e4m3": (ml_dtypes.float8_e4m3fn, 7), "e5m2": (ml_dtypes.float8_e5m2, 14)}[fmt]
    v = np.moveaxis(np.asarray(x, np.float32).astype(ml_dtypes.bfloat16).astype(np.float64), axis, -1)
    blocks = v.reshape(v.shape[:-1] + (-1, 32))
    amax = np.abs(blocks).max(-1, keepdims=True)
    byte = np.maximum(np.where(amax > 0, np.frexp(amax)[1] - 1 + 127, 0) - down, 1)
    scale = np.exp2(byte - 127.0)
    codes = (blocks / scale).astype(np.float32).astype(dtype).astype(np.float64)
    return np.moveaxis((codes * scale).reshape(v.shape), -1, axis)


WIDE = False


def mx_kscale(k):
    if not WIDE:
        return np.ones(k)
    levels = np.array([20, -20, 10, -10, 0])
    a = np.random.permutation(np.resize(levels, k // 512 * 4)).reshape(k // 512, 4)
    idx = np.arange(k)
    return np.exp2(a[idx // 512, idx % 128 // 32])


BF16 = ml_dtypes.bfloat16


def bf(x):
    return np.asarray(x, np.float32).astype(BF16)


def f64(x):
    return np.asarray(x).astype(np.float64)


B, S, D_IN, D_OUT, R = 2, 2048, 1024, 512, 128
LORA_SCALE = 2.0


def setup_inputs():
    u = mx_kscale(D_OUT)
    x = np.random.standard_normal((B, S, D_IN))
    weight = np.random.standard_normal((D_OUT, D_IN)) * 1.0 / np.sqrt(D_IN) / u[:, None]
    bias = np.random.standard_normal(D_OUT) * 0.5
    lora_left = np.random.standard_normal((D_OUT, R)) * 0.5 / np.sqrt(R) / u[:, None]
    lora_right = np.random.standard_normal((R, D_IN)) * 0.5 / np.sqrt(D_IN)
    g = np.random.standard_normal((B, S, D_OUT)) * np.exp2(np.random.randint(-12, 1, (B, S, 1))) * 16.0 * u
    return {"x": bf(x), "weight": bf(weight), "bias": bf(bias),
            "lora_left": bf(lora_left), "lora_right": bf(lora_right), "grad_out": bf(g)}


def reference(x, weight, bias, lora_left, lora_right, grad_out):
    g = mxq(f64(grad_out), 2, "e5m2")
    main = g @ mxq(f64(weight), 0, "e4m3")
    t = g @ mxq(f64(lora_left), 0, "e4m3")
    return main + LORA_SCALE * (t @ f64(lora_right))

@@ -1,0 +1,235 @@
+from contextlib import ExitStack
+
+import concourse.mybir as mybir
+from concourse.masks import make_identity
+
+F32 = mybir.dt.float32
+BF16 = mybir.dt.bfloat16
+U32 = mybir.dt.uint32
+U8 = mybir.dt.uint8
+E4X4 = mybir.dt.float8_e4m3fn_x4
+E5X4 = mybir.dt.float8_e5m2_x4
+ADD = mybir.AluOpType.add
+MULT = mybir.AluOpType.mult
+
+P = 128
+TOKENS = 4096
+K = 512
+D_IN = 1024
+RANK = 128
+CHUNK = 512
+N_CHUNKS = TOKENS // CHUNK
+S = CHUNK // P
+HALF = 512
+H = D_IN // HALF
+
+FLOPS = 2 * TOKENS * (K * D_IN + K * RANK + RANK * D_IN)
+BYTES = 2 * (TOKENS * K + K * D_IN + K * RANK + RANK * D_IN) + 4 * TOKENS * D_IN
+
+
+def tile_loralinear_t_kernel(tc, x, weight, bias, lora_left, lora_right, grad_out, out):
+    nc = tc.nc
+    g = grad_out.flatten_outer_dims()
+    o = out.flatten_outer_dims()
+    with ExitStack() as ctx:
+        const = ctx.enter_context(tc.tile_pool(name="const", bufs=1))
+        grp_pool = ctx.enter_context(tc.tile_pool(name="grp", bufs=2))
+        code_pool = ctx.enter_context(tc.tile_pool(name="codes", bufs=3))
+        t_pool = ctx.enter_context(tc.tile_pool(name="tT", bufs=2))
+        o_pool = ctx.enter_context(tc.tile_pool(name="o", bufs=6))
+        psum = ctx.enter_context(tc.psum_pool(name="psum", bufs=8))
+
+        g_raw = const.tile([P, N_CHUNKS, S * K], BF16)
+        w_raw = const.tile([P, 4, D_IN], BF16)
+        w_grp = const.tile([P, D_IN, 4], BF16, align_bytes=64)
+        w_codes = const.tile([P, D_IN], U32, align_bytes=64)
+        w_scales = const.tile([P, D_IN], U8, align_bytes=64)
+        l_raw = const.tile([P, 4, RANK], BF16)
+        l_grp = const.tile([P, RANK, 4], BF16, align_bytes=64)
+        l_codes = const.tile([P, RANK], U32, align_bytes=64)
+        l_scales = const.tile([P, RANK], U8, align_bytes=64)
+        r_raw = const.tile([P, D_IN], BF16)
+        r32 = const.tile([P, D_IN], F32)
+        ident = const.tile([P, P], F32)
+
+        state = {}
+
+        def load_g(c, s0, s1):
+            nc.sync.dma_start(
+                out=g_raw[:, c, s0 * K : s1 * K].rearrange("p (s k) -> p s k", k=K),
+                in_=g[c * CHUNK + s0 * P : c * CHUNK + s1 * P, :].rearrange("(s p) k -> p s k", p=P),
+            )
+
+        def regroup(dst, src):
+            nc.vector.tensor_copy(
+                out=dst.rearrange("p (c i) t -> p c t i", i=4),
+                in_=src.rearrange("p t (c i) -> p c t i", i=4),
+            )
+
+        def transposes(c, j):
+            tr = psum.tile([P, 2, 2, P], F32, tag="bank")
+            words = g_raw[:, c, :].bitcast(F32)
+            for sl in range(2):
+                for u in range(2):
+                    w0 = (2 * j + sl) * 256 + u * P
+                    nc.tensor.transpose(tr[:, sl, u, :], words[:, w0 : w0 + P], ident[:])
+            return tr
+
+        def new_chunk(c):
+            grp = grp_pool.tile([P, CHUNK * 4], BF16, align_bytes=64)
+            codes = code_pool.tile([P, CHUNK], U32, align_bytes=64)
+            scales = code_pool.tile([P, CHUNK], U8, align_bytes=64)
+            state[c] = {"grp": grp, "codes": codes, "scales": scales}
+
+        def copy_out(c, j, tr, on_vector):
+            dst = state[c]["grp"][:].bitcast(F32)[:, j * 512 : (j + 1) * 512]
+            dst = dst.rearrange("q (s p u) -> q s p u", s=2, u=2)
+            src = tr[:].rearrange("q s u p -> q s p u")
+            if on_vector:
+                nc.vector.tensor_copy(out=dst, in_=src)
+            else:
+                nc.scalar.copy(out=dst, in_=src)
+
+        def quantise(c, t0, t1):
+            st = state[c]
+            nc.vector.quantize_mx(
+                out=st["codes"][:, t0:t1].bitcast(E5X4),
+                scales=st["scales"][:, t0:t1],
+                in_=st["grp"][:, 4 * t0 : 4 * t1],
+            )
+
+        def make_t(c, cuts):
+            st = state[c]
+            tt = psum.tile([P, CHUNK], F32, tag="bank")
+            nc.tensor.matmul_mx(
+                out=tt[:],
+                lhsT=l_codes[:].bitcast(E4X4),
+                lhsT_scale=l_scales[:],
+                rhs=st["codes"][:].bitcast(E5X4),
+                rhs_scale=st["scales"][:],
+                start=True,
+                stop=True,
+            )
+            t_sb = t_pool.tile([P, CHUNK], F32)
+            for a, b in zip(cuts[:-1], cuts[1:]):
+                nc.scalar.copy(out=t_sb[:, a:b], in_=tt[:, a:b])
+            st["t"] = t_sb
+
+        def main_pass(c, s, h):
+            st = state[c]
+            acc = psum.tile([P, HALF], F32, tag="bank")
+            nc.tensor.matmul_mx(
+                out=acc[:],
+                lhsT=st["codes"][:, s * P : (s + 1) * P].bitcast(E5X4),
+                lhsT_scale=st["scales"][:, s * P : (s + 1) * P],
+                rhs=w_codes[:, h * HALF : (h + 1) * HALF].bitcast(E4X4),
+                rhs_scale=w_scales[:, h * HALF : (h + 1) * HALF],
+                start=True,
+                stop=True,
+            )
+            return acc
+
+        def low_pass(c, s, h):
+            acc = psum.tile([P, HALF], F32, tag="bank")
+            nc.tensor.matmul(
+                out=acc[:],
+                lhsT=state[c]["t"][:, s * P : (s + 1) * P],
+                rhs=r32[:, h * HALF : (h + 1) * HALF],
+                start=True,
+                stop=True,
+            )
+            return acc
+
+        def first(c, s, product):
+            o_sb = o_pool.tile([P, D_IN], F32)
+            state[(c, s)] = o_sb
+            accs = [product(c, s, h) for h in range(H)]
+            for h in range(H):
+                nc.scalar.copy(out=o_sb[:, h * HALF : (h + 1) * HALF], in_=accs[h][:])
+
+        def second(c, s, product):
+            o_sb = state[(c, s)]
+            rows = o[c * CHUNK + s * P : c * CHUNK + (s + 1) * P, :]
+            last = c == N_CHUNKS - 1 and s == S - 1
+            accs = [product(c, s, h) for h in range(H)]
+            for h in range(H):
+                cols = slice(h * HALF, (h + 1) * HALF)
+                nc.vector.tensor_tensor(out=o_sb[:, cols], in0=accs[h][:], in1=o_sb[:, cols], op=ADD)
+                if last:
+                    nc.sync.dma_start(out=rows[:, cols], in_=o_sb[:, cols])
+            if not last:
+                nc.sync.dma_start(out=rows, in_=o_sb[:])
+
+        with tc.manual_schedule():
+            load_g(0, 0, 2)
+            load_g(0, 2, 4)
+            nc.sync.dma_start(
+                out=l_raw[:].rearrange("q (u e) r -> q u (e r)", u=2),
+                in_=lora_left.rearrange("(u q e) r -> q u (e r)", u=2, e=2),
+            )
+            nc.sync.dma_start(out=r_raw[:], in_=lora_right)
+            load_g(1, 0, S)
+            w_view = weight.rearrange("(u q e) n -> u q (e n)", u=2, e=2)
+            for u in range(2):
+                nc.sync.dma_start(
+                    out=w_raw[:, 2 * u : 2 * u + 2, :].rearrange("q e n -> q (e n)"), in_=w_view[u]
+                )
+            for c in range(2, N_CHUNKS):
+                load_g(c, 0, S)
+
+            make_identity(nc, ident[:])
+            nc.gpsimd.tensor_scalar(out=r32[:], in0=r_raw[:], scalar1=2.0, scalar2=0.0, op0=MULT, op1=ADD)
+
+            new_chunk(0)
+            tr = transposes(0, 0)
+            copy_out(0, 0, tr, True)
+            tr = transposes(0, 1)
+            copy_out(0, 1, tr, False)
+            regroup(l_grp[:], l_raw[:])
+            quantise(0, 0, 256)
+            nc.vector.quantize_mx(
+                out=l_codes[:].bitcast(E4X4), scales=l_scales[:], in_=l_grp[:].rearrange("p r t -> p (r t)")
+            )
+            quantise(0, 256, 512)
+            make_t(0, [0, P, CHUNK])
+
+            new_chunk(1)
+            tr = transposes(1, 0)
+            copy_out(1, 0, tr, True)
+            tr = transposes(1, 1)
+            copy_out(1, 1, tr, False)
+
+            first(0, 0, low_pass)
+            first(0, 1, low_pass)
+            for h in range(H):
+                regroup(w_grp[:, h * HALF : (h + 1) * HALF, :], w_raw[:, :, h * HALF : (h + 1) * HALF])
+            for h in range(H):
+                nc.vector.quantize_mx(
+                    out=w_codes[:, h * HALF : (h + 1) * HALF].bitcast(E4X4),
+                    scales=w_scales[:, h * HALF : (h + 1) * HALF],
+                    in_=w_grp[:, h * HALF : (h + 1) * HALF, :].rearrange("p n t -> p (n t)"),
+                )
+            quantise(1, 0, CHUNK)
+            second(0, 0, main_pass)
+            first(0, 2, low_pass)
+            second(0, 1, main_pass)
+            first(0, 3, low_pass)
+            make_t(1, [0, CHUNK])
+            second(0, 2, main_pass)
+            second(0, 3, main_pass)
+
+            for c in range(1, N_CHUNKS):
+                more = c + 1 < N_CHUNKS
+                if more:
+                    new_chunk(c + 1)
+                    tr = transposes(c + 1, 0)
+                    copy_out(c + 1, 0, tr, True)
+                    tr = transposes(c + 1, 1)
+                    copy_out(c + 1, 1, tr, False)
+                for s in range(S):
+                    first(c, s, main_pass)
+                    second(c, s, low_pass)
+                    if more and s == 0:
+                        quantise(c + 1, 0, CHUNK)
+                    if more and s == 1:
+                        make_t(c + 1, [0, CHUNK])

@@ -35,11 +35,12 @@ def tile_loralinear_t_kernel(tc, x, weight, bias, lora_left, lora_right, grad_ou
         const = ctx.enter_context(tc.tile_pool(name="const", bufs=1))
         grp_pool = ctx.enter_context(tc.tile_pool(name="grp", bufs=2))
         code_pool = ctx.enter_context(tc.tile_pool(name="codes", bufs=3))
+        x_pool = ctx.enter_context(tc.tile_pool(name="x", bufs=3))
         t_pool = ctx.enter_context(tc.tile_pool(name="tT", bufs=2))
         o_pool = ctx.enter_context(tc.tile_pool(name="o", bufs=6))
         psum = ctx.enter_context(tc.psum_pool(name="psum", bufs=8))
 
-        g_raw = const.tile([P, N_CHUNKS, S * K], BF16)
+        g_raw = const.tile([P, 1, S * K], BF16)
         w_raw = const.tile([P, 4, D_IN], BF16)
         w_grp = const.tile([P, D_IN, 4], BF16, align_bytes=64)
         w_codes = const.tile([P, D_IN], U32, align_bytes=64)
@@ -59,6 +60,18 @@ def tile_loralinear_t_kernel(tc, x, weight, bias, lora_left, lora_right, grad_ou
                 out=g_raw[:, c, s0 * K : s1 * K].rearrange("p (s k) -> p s k", k=K),
                 in_=g[c * CHUNK + s0 * P : c * CHUNK + s1 * P, :].rearrange("(s p) k -> p s k", p=P),
             )
+
+        half_rows = g.rearrange("t (u r) -> (t u) r", u=2)
+
+        def load_x(c):
+            xt = x_pool.tile([P, CHUNK * 4], BF16, align_bytes=64)
+            src = half_rows[c * 2 * CHUNK : (c + 1) * 2 * CHUNK, :].rearrange("(j b) (i w) -> i b j w", b=32, i=4)
+            for i in range(4):
+                nc.sync.dma_start(out=xt[32 * i : 32 * i + 32, :].rearrange("b (j w) -> b j w", w=64), in_=src[i])
+            state[("x", c)] = xt
+
+        def block_transposes(c):
+            nc.vector.transpose(out=state[c]["grp"][:].bitcast(F32), in_=state[("x", c)][:].bitcast(F32))
 
         def regroup(dst, src):
             nc.vector.tensor_copy(
@@ -168,14 +181,13 @@ def tile_loralinear_t_kernel(tc, x, weight, bias, lora_left, lora_right, grad_ou
                 in_=lora_left.rearrange("(u q e) r -> q u (e r)", u=2, e=2),
             )
             nc.sync.dma_start(out=r_raw[:], in_=lora_right)
-            load_g(1, 0, S)
             w_view = weight.rearrange("(u q e) n -> u q (e n)", u=2, e=2)
             for u in range(2):
                 nc.sync.dma_start(
                     out=w_raw[:, 2 * u : 2 * u + 2, :].rearrange("q e n -> q (e n)"), in_=w_view[u]
                 )
-            for c in range(2, N_CHUNKS):
-                load_g(c, 0, S)
+            load_x(1)
+            load_x(2)
 
             make_identity(nc, ident[:])
             nc.gpsimd.tensor_scalar(out=r32[:], in0=r_raw[:], scalar1=2.0, scalar2=0.0, op0=MULT, op1=ADD)
@@ -193,12 +205,6 @@ def tile_loralinear_t_kernel(tc, x, weight, bias, lora_left, lora_right, grad_ou
             quantise(0, 256, 512)
             make_t(0, [0, P, CHUNK])
 
-            new_chunk(1)
-            tr = transposes(1, 0)
-            copy_out(1, 0, tr, True)
-            tr = transposes(1, 1)
-            copy_out(1, 1, tr, False)
-
             first(0, 0, low_pass)
             first(0, 1, low_pass)
             for h in range(H):
@@ -209,8 +215,10 @@ def tile_loralinear_t_kernel(tc, x, weight, bias, lora_left, lora_right, grad_ou
                     scales=w_scales[:, h * HALF : (h + 1) * HALF],
                     in_=w_grp[:, h * HALF : (h + 1) * HALF, :].rearrange("p n t -> p (n t)"),
                 )
-            quantise(1, 0, CHUNK)
+            new_chunk(1)
+            block_transposes(1)
             second(0, 0, main_pass)
+            quantise(1, 0, CHUNK)
             first(0, 2, low_pass)
             second(0, 1, main_pass)
             first(0, 3, low_pass)
@@ -222,10 +230,9 @@ def tile_loralinear_t_kernel(tc, x, weight, bias, lora_left, lora_right, grad_ou
                 more = c + 1 < N_CHUNKS
                 if more:
                     new_chunk(c + 1)
-                    tr = transposes(c + 1, 0)
-                    copy_out(c + 1, 0, tr, True)
-                    tr = transposes(c + 1, 1)
-                    copy_out(c + 1, 1, tr, False)
+                    block_transposes(c + 1)
+                if c + 2 < N_CHUNKS:
+                    load_x(c + 2)
                 for s in range(S):
                     first(c, s, main_pass)
                     second(c, s, low_pass)

@@ -22,6 +22,7 @@ N_CHUNKS = TOKENS // CHUNK
 S = CHUNK // P
 HALF = 512
 H = D_IN // HALF
+FIRST_VECTOR_CHUNK = 4
 
 FLOPS = 2 * TOKENS * (K * D_IN + K * RANK + RANK * D_IN)
 BYTES = 2 * (TOKENS * K + K * D_IN + K * RANK + RANK * D_IN) + 4 * TOKENS * D_IN
@@ -35,12 +36,12 @@ def tile_loralinear_t_kernel(tc, x, weight, bias, lora_left, lora_right, grad_ou
         const = ctx.enter_context(tc.tile_pool(name="const", bufs=1))
         grp_pool = ctx.enter_context(tc.tile_pool(name="grp", bufs=2))
         code_pool = ctx.enter_context(tc.tile_pool(name="codes", bufs=3))
-        x_pool = ctx.enter_context(tc.tile_pool(name="x", bufs=3))
+        x_pool = ctx.enter_context(tc.tile_pool(name="x", bufs=N_CHUNKS - FIRST_VECTOR_CHUNK))
         t_pool = ctx.enter_context(tc.tile_pool(name="tT", bufs=2))
-        o_pool = ctx.enter_context(tc.tile_pool(name="o", bufs=6))
+        o_pool = ctx.enter_context(tc.tile_pool(name="o", bufs=8))
         psum = ctx.enter_context(tc.psum_pool(name="psum", bufs=8))
 
-        g_raw = const.tile([P, 1, S * K], BF16)
+        g_raw = const.tile([P, FIRST_VECTOR_CHUNK, S * K], BF16)
         w_raw = const.tile([P, 4, D_IN], BF16)
         w_grp = const.tile([P, D_IN, 4], BF16, align_bytes=64)
         w_codes = const.tile([P, D_IN], U32, align_bytes=64)
@@ -63,12 +64,19 @@ def tile_loralinear_t_kernel(tc, x, weight, bias, lora_left, lora_right, grad_ou
 
         half_rows = g.rearrange("t (u r) -> (t u) r", u=2)
 
-        def load_x(c):
-            xt = x_pool.tile([P, CHUNK * 4], BF16, align_bytes=64)
-            src = half_rows[c * 2 * CHUNK : (c + 1) * 2 * CHUNK, :].rearrange("(j b) (i w) -> i b j w", b=32, i=4)
-            for i in range(4):
-                nc.sync.dma_start(out=xt[32 * i : 32 * i + 32, :].rearrange("b (j w) -> b j w", w=64), in_=src[i])
-            state[("x", c)] = xt
+        pending = [(c, i) for c in range(FIRST_VECTOR_CHUNK, N_CHUNKS) for i in range(4)]
+        cursor = [0]
+
+        def load_x(count):
+            for c, i in pending[cursor[0] : cursor[0] + count]:
+                if i == 0:
+                    xt = x_pool.tile([P, CHUNK * 4], BF16, align_bytes=64)
+                    state[("x", c)] = xt
+                src = half_rows[c * 2 * CHUNK : (c + 1) * 2 * CHUNK, :].rearrange("(j b) (i w) -> i b j w", b=32, i=4)
+                nc.sync.dma_start(
+                    out=state[("x", c)][32 * i : 32 * i + 32, :].rearrange("b (j w) -> b j w", w=64), in_=src[i]
+                )
+            cursor[0] += count
 
         def block_transposes(c):
             nc.vector.transpose(out=state[c]["grp"][:].bitcast(F32), in_=state[("x", c)][:].bitcast(F32))
@@ -160,11 +168,20 @@ def tile_loralinear_t_kernel(tc, x, weight, bias, lora_left, lora_right, grad_ou
             for h in range(H):
                 nc.scalar.copy(out=o_sb[:, h * HALF : (h + 1) * HALF], in_=accs[h][:])
 
-        def second(c, s, product):
+        def pe_prepare(c):
+            tr = transposes(c, 0)
+            copy_out(c, 0, tr, True)
+            tr = transposes(c, 1)
+            copy_out(c, 1, tr, False)
+
+        def second(c, s, product, prepare=None):
             o_sb = state[(c, s)]
             rows = o[c * CHUNK + s * P : c * CHUNK + (s + 1) * P, :]
             last = c == N_CHUNKS - 1 and s == S - 1
-            accs = [product(c, s, h) for h in range(H)]
+            accs = [product(c, s, 0)]
+            if prepare is not None:
+                pe_prepare(prepare)
+            accs.append(product(c, s, 1))
             for h in range(H):
                 cols = slice(h * HALF, (h + 1) * HALF)
                 nc.vector.tensor_tensor(out=o_sb[:, cols], in0=accs[h][:], in1=o_sb[:, cols], op=ADD)
@@ -172,6 +189,7 @@ def tile_loralinear_t_kernel(tc, x, weight, bias, lora_left, lora_right, grad_ou
                     nc.sync.dma_start(out=rows[:, cols], in_=o_sb[:, cols])
             if not last:
                 nc.sync.dma_start(out=rows, in_=o_sb[:])
+            load_x(1)
 
         with tc.manual_schedule():
             load_g(0, 0, 2)
@@ -181,13 +199,15 @@ def tile_loralinear_t_kernel(tc, x, weight, bias, lora_left, lora_right, grad_ou
                 in_=lora_left.rearrange("(u q e) r -> q u (e r)", u=2, e=2),
             )
             nc.sync.dma_start(out=r_raw[:], in_=lora_right)
+            load_g(1, 0, S)
             w_view = weight.rearrange("(u q e) n -> u q (e n)", u=2, e=2)
             for u in range(2):
                 nc.sync.dma_start(
                     out=w_raw[:, 2 * u : 2 * u + 2, :].rearrange("q e n -> q (e n)"), in_=w_view[u]
                 )
-            load_x(1)
-            load_x(2)
+            for c in range(2, FIRST_VECTOR_CHUNK):
+                load_g(c, 0, S)
+            load_x(4)
 
             make_identity(nc, ident[:])
             nc.gpsimd.tensor_scalar(out=r32[:], in0=r_raw[:], scalar1=2.0, scalar2=0.0, op0=MULT, op1=ADD)
@@ -204,6 +224,8 @@ def tile_loralinear_t_kernel(tc, x, weight, bias, lora_left, lora_right, grad_ou
             )
             quantise(0, 256, 512)
             make_t(0, [0, P, CHUNK])
+            new_chunk(1)
+            pe_prepare(1)
 
             first(0, 0, low_pass)
             first(0, 1, low_pass)
@@ -215,8 +237,6 @@ def tile_loralinear_t_kernel(tc, x, weight, bias, lora_left, lora_right, grad_ou
                     scales=w_scales[:, h * HALF : (h + 1) * HALF],
                     in_=w_grp[:, h * HALF : (h + 1) * HALF, :].rearrange("p n t -> p (n t)"),
                 )
-            new_chunk(1)
-            block_transposes(1)
             second(0, 0, main_pass)
             quantise(1, 0, CHUNK)
             first(0, 2, low_pass)
@@ -228,14 +248,14 @@ def tile_loralinear_t_kernel(tc, x, weight, bias, lora_left, lora_right, grad_ou
 
             for c in range(1, N_CHUNKS):
                 more = c + 1 < N_CHUNKS
+                on_pe = more and c + 1 < FIRST_VECTOR_CHUNK
                 if more:
                     new_chunk(c + 1)
+                if more and not on_pe:
                     block_transposes(c + 1)
-                if c + 2 < N_CHUNKS:
-                    load_x(c + 2)
                 for s in range(S):
                     first(c, s, main_pass)
-                    second(c, s, low_pass)
+                    second(c, s, low_pass, c + 1 if on_pe and s == 0 else None)
                     if more and s == 0:
                         quantise(c + 1, 0, CHUNK)
                     if more and s == 1:

@@ -22,7 +22,6 @@ N_CHUNKS = TOKENS // CHUNK
 S = CHUNK // P
 HALF = 512
 H = D_IN // HALF
-FIRST_VECTOR_CHUNK = 4
 
 FLOPS = 2 * TOKENS * (K * D_IN + K * RANK + RANK * D_IN)
 BYTES = 2 * (TOKENS * K + K * D_IN + K * RANK + RANK * D_IN) + 4 * TOKENS * D_IN
@@ -36,12 +35,11 @@ def tile_loralinear_t_kernel(tc, x, weight, bias, lora_left, lora_right, grad_ou
         const = ctx.enter_context(tc.tile_pool(name="const", bufs=1))
         grp_pool = ctx.enter_context(tc.tile_pool(name="grp", bufs=2))
         code_pool = ctx.enter_context(tc.tile_pool(name="codes", bufs=3))
-        x_pool = ctx.enter_context(tc.tile_pool(name="x", bufs=N_CHUNKS - FIRST_VECTOR_CHUNK))
         t_pool = ctx.enter_context(tc.tile_pool(name="tT", bufs=2))
-        o_pool = ctx.enter_context(tc.tile_pool(name="o", bufs=8))
+        o_pool = ctx.enter_context(tc.tile_pool(name="o", bufs=10))
         psum = ctx.enter_context(tc.psum_pool(name="psum", bufs=8))
 
-        g_raw = const.tile([P, FIRST_VECTOR_CHUNK, S * K], BF16)
+        g_raw = const.tile([P, N_CHUNKS, S * K], BF16)
         w_raw = const.tile([P, 4, D_IN], BF16)
         w_grp = const.tile([P, D_IN, 4], BF16, align_bytes=64)
         w_codes = const.tile([P, D_IN], U32, align_bytes=64)
@@ -62,64 +60,49 @@ def tile_loralinear_t_kernel(tc, x, weight, bias, lora_left, lora_right, grad_ou
                 in_=g[c * CHUNK + s0 * P : c * CHUNK + s1 * P, :].rearrange("(s p) k -> p s k", p=P),
             )
 
-        half_rows = g.rearrange("t (u r) -> (t u) r", u=2)
-
-        pending = [(c, i) for c in range(FIRST_VECTOR_CHUNK, N_CHUNKS) for i in range(4)]
-        cursor = [0]
-
-        def load_x(count):
-            for c, i in pending[cursor[0] : cursor[0] + count]:
-                if i == 0:
-                    xt = x_pool.tile([P, CHUNK * 4], BF16, align_bytes=64)
-                    state[("x", c)] = xt
-                src = half_rows[c * 2 * CHUNK : (c + 1) * 2 * CHUNK, :].rearrange("(j b) (i w) -> i b j w", b=32, i=4)
-                nc.sync.dma_start(
-                    out=state[("x", c)][32 * i : 32 * i + 32, :].rearrange("b (j w) -> b j w", w=64), in_=src[i]
-                )
-            cursor[0] += count
-
-        def block_transposes(c):
-            nc.vector.transpose(out=state[c]["grp"][:].bitcast(F32), in_=state[("x", c)][:].bitcast(F32))
-
         def regroup(dst, src):
             nc.vector.tensor_copy(
                 out=dst.rearrange("p (c i) t -> p c t i", i=4),
                 in_=src.rearrange("p t (c i) -> p c t i", i=4),
             )
 
-        def transposes(c, j):
-            tr = psum.tile([P, 2, 2, P], F32, tag="bank")
+        def one_transpose(c, i):
+            if c >= N_CHUNKS:
+                return
+            if i == 0:
+                grp = grp_pool.tile([P, CHUNK * 4], BF16, align_bytes=64)
+                codes = code_pool.tile([P, CHUNK], U32, align_bytes=64)
+                scales = code_pool.tile([P, CHUNK], U8, align_bytes=64)
+                state[c] = {"grp": grp, "codes": codes, "scales": scales}
+            if i % 4 == 0:
+                tr = psum.tile([P, 2, 2, P], F32, tag="bank")
+                state[c]["tr"] = tr
+            tr = state[c]["tr"]
             words = g_raw[:, c, :].bitcast(F32)
-            for sl in range(2):
-                for u in range(2):
-                    w0 = (2 * j + sl) * 256 + u * P
-                    nc.tensor.transpose(tr[:, sl, u, :], words[:, w0 : w0 + P], ident[:])
-            return tr
+            nc.tensor.transpose(tr[:, (i % 4) // 2, i % 2, :], words[:, i * P : (i + 1) * P], ident[:])
+            if i % 4 == 3:
+                j = i // 4
+                dst = state[c]["grp"][:].bitcast(F32)[:, j * 512 : (j + 1) * 512]
+                dst = dst.rearrange("q (s p u) -> q s p u", s=2, u=2)
+                src = tr[:].rearrange("q s u p -> q s p u")
+                if j == 0:
+                    nc.vector.tensor_copy(out=dst, in_=src)
+                else:
+                    nc.scalar.copy(out=dst, in_=src)
 
-        def new_chunk(c):
-            grp = grp_pool.tile([P, CHUNK * 4], BF16, align_bytes=64)
-            codes = code_pool.tile([P, CHUNK], U32, align_bytes=64)
-            scales = code_pool.tile([P, CHUNK], U8, align_bytes=64)
-            state[c] = {"grp": grp, "codes": codes, "scales": scales}
-
-        def copy_out(c, j, tr, on_vector):
-            dst = state[c]["grp"][:].bitcast(F32)[:, j * 512 : (j + 1) * 512]
-            dst = dst.rearrange("q (s p u) -> q s p u", s=2, u=2)
-            src = tr[:].rearrange("q s u p -> q s p u")
-            if on_vector:
-                nc.vector.tensor_copy(out=dst, in_=src)
-            else:
-                nc.scalar.copy(out=dst, in_=src)
-
-        def quantise(c, t0, t1):
+        def quantise(c, j):
+            if c >= N_CHUNKS:
+                return
             st = state[c]
             nc.vector.quantize_mx(
-                out=st["codes"][:, t0:t1].bitcast(E5X4),
-                scales=st["scales"][:, t0:t1],
-                in_=st["grp"][:, 4 * t0 : 4 * t1],
+                out=st["codes"][:, j * 256 : (j + 1) * 256].bitcast(E5X4),
+                scales=st["scales"][:, j * 256 : (j + 1) * 256],
+                in_=st["grp"][:, j * 1024 : (j + 1) * 1024],
             )
 
         def make_t(c, cuts):
+            if c >= N_CHUNKS:
+                return
             st = state[c]
             tt = psum.tile([P, CHUNK], F32, tag="bank")
             nc.tensor.matmul_mx(
@@ -161,35 +144,34 @@ def tile_loralinear_t_kernel(tc, x, weight, bias, lora_left, lora_right, grad_ou
             )
             return acc
 
-        def first(c, s, product):
-            o_sb = o_pool.tile([P, D_IN], F32)
-            state[(c, s)] = o_sb
-            accs = [product(c, s, h) for h in range(H)]
-            for h in range(H):
-                nc.scalar.copy(out=o_sb[:, h * HALF : (h + 1) * HALF], in_=accs[h][:])
+        def first(c, i, product):
+            s, h = divmod(i, H)
+            if h == 0:
+                o_sb = o_pool.tile([P, D_IN], F32)
+                state[(c, s)] = o_sb
+            acc = product(c, s, h)
+            nc.scalar.copy(out=state[(c, s)][:, h * HALF : (h + 1) * HALF], in_=acc[:])
 
-        def pe_prepare(c):
-            tr = transposes(c, 0)
-            copy_out(c, 0, tr, True)
-            tr = transposes(c, 1)
-            copy_out(c, 1, tr, False)
-
-        def second(c, s, product, prepare=None):
+        def second(c, i, product):
+            s, h = divmod(i, H)
             o_sb = state[(c, s)]
             rows = o[c * CHUNK + s * P : c * CHUNK + (s + 1) * P, :]
             last = c == N_CHUNKS - 1 and s == S - 1
-            accs = [product(c, s, 0)]
-            if prepare is not None:
-                pe_prepare(prepare)
-            accs.append(product(c, s, 1))
-            for h in range(H):
-                cols = slice(h * HALF, (h + 1) * HALF)
-                nc.vector.tensor_tensor(out=o_sb[:, cols], in0=accs[h][:], in1=o_sb[:, cols], op=ADD)
-                if last:
-                    nc.sync.dma_start(out=rows[:, cols], in_=o_sb[:, cols])
-            if not last:
+            cols = slice(h * HALF, (h + 1) * HALF)
+            acc = product(c, s, h)
+            nc.vector.tensor_tensor(out=o_sb[:, cols], in0=acc[:], in1=o_sb[:, cols], op=ADD)
+            if last:
+                nc.sync.dma_start(out=rows[:, cols], in_=o_sb[:, cols])
+            elif h == H - 1:
                 nc.sync.dma_start(out=rows, in_=o_sb[:])
-            load_x(1)
+
+        def plain_bunch(c, place):
+            for i in range(S * H):
+                one_transpose(c + 2, i)
+                place(c, i, low_pass)
+                if i == 5:
+                    quantise(c + 2, 0)
+            quantise(c + 2, 1)
 
         with tc.manual_schedule():
             load_g(0, 0, 2)
@@ -200,35 +182,31 @@ def tile_loralinear_t_kernel(tc, x, weight, bias, lora_left, lora_right, grad_ou
             )
             nc.sync.dma_start(out=r_raw[:], in_=lora_right)
             load_g(1, 0, S)
+            load_g(2, 0, S)
             w_view = weight.rearrange("(u q e) n -> u q (e n)", u=2, e=2)
             for u in range(2):
                 nc.sync.dma_start(
                     out=w_raw[:, 2 * u : 2 * u + 2, :].rearrange("q e n -> q (e n)"), in_=w_view[u]
                 )
-            for c in range(2, FIRST_VECTOR_CHUNK):
+            for c in range(3, N_CHUNKS):
                 load_g(c, 0, S)
-            load_x(4)
 
             make_identity(nc, ident[:])
             nc.gpsimd.tensor_scalar(out=r32[:], in0=r_raw[:], scalar1=2.0, scalar2=0.0, op0=MULT, op1=ADD)
 
-            new_chunk(0)
-            tr = transposes(0, 0)
-            copy_out(0, 0, tr, True)
-            tr = transposes(0, 1)
-            copy_out(0, 1, tr, False)
+            for i in range(8):
+                one_transpose(0, i)
             regroup(l_grp[:], l_raw[:])
-            quantise(0, 0, 256)
+            quantise(0, 0)
             nc.vector.quantize_mx(
                 out=l_codes[:].bitcast(E4X4), scales=l_scales[:], in_=l_grp[:].rearrange("p r t -> p (r t)")
             )
-            quantise(0, 256, 512)
+            quantise(0, 1)
             make_t(0, [0, P, CHUNK])
-            new_chunk(1)
-            pe_prepare(1)
-
-            first(0, 0, low_pass)
-            first(0, 1, low_pass)
+            for i in range(8):
+                one_transpose(1, i)
+            quantise(1, 0)
+            quantise(1, 1)
             for h in range(H):
                 regroup(w_grp[:, h * HALF : (h + 1) * HALF, :], w_raw[:, :, h * HALF : (h + 1) * HALF])
             for h in range(H):
@@ -237,26 +215,16 @@ def tile_loralinear_t_kernel(tc, x, weight, bias, lora_left, lora_right, grad_ou
                     scales=w_scales[:, h * HALF : (h + 1) * HALF],
                     in_=w_grp[:, h * HALF : (h + 1) * HALF, :].rearrange("p n t -> p (n t)"),
                 )
-            second(0, 0, main_pass)
-            quantise(1, 0, CHUNK)
-            first(0, 2, low_pass)
-            second(0, 1, main_pass)
-            first(0, 3, low_pass)
-            make_t(1, [0, CHUNK])
-            second(0, 2, main_pass)
-            second(0, 3, main_pass)
 
-            for c in range(1, N_CHUNKS):
-                more = c + 1 < N_CHUNKS
-                on_pe = more and c + 1 < FIRST_VECTOR_CHUNK
-                if more:
-                    new_chunk(c + 1)
-                if more and not on_pe:
-                    block_transposes(c + 1)
-                for s in range(S):
-                    first(c, s, main_pass)
-                    second(c, s, low_pass, c + 1 if on_pe and s == 0 else None)
-                    if more and s == 0:
-                        quantise(c + 1, 0, CHUNK)
-                    if more and s == 1:
-                        make_t(c + 1, [0, CHUNK])
+            plain_bunch(0, first)
+            make_t(1, [0, CHUNK])
+            for i in range(S * H):
+                second(0, i, main_pass)
+                first(1, i, main_pass)
+            make_t(2, [0, CHUNK])
+            plain_bunch(1, second)
+            for c in range(2, N_CHUNKS):
+                for i in range(S * H):
+                    first(c, i, main_pass)
+                make_t(c + 1, [0, CHUNK])
+                plain_bunch(c, second)

@@ -7,6 +7,7 @@ F32 = mybir.dt.float32
 BF16 = mybir.dt.bfloat16
 U32 = mybir.dt.uint32
 U8 = mybir.dt.uint8
+I32 = mybir.dt.int32
 E4X4 = mybir.dt.float8_e4m3fn_x4
 E5X4 = mybir.dt.float8_e5m2_x4
 ADD = mybir.AluOpType.add
@@ -22,6 +23,8 @@ N_CHUNKS = TOKENS // CHUNK
 S = CHUNK // P
 HALF = 512
 H = D_IN // HALF
+GROUPS_FIRST = [(0, 1), (1, 3), (3, 4)]
+GROUPS = [(0, 2), (2, 4)]
 
 FLOPS = 2 * TOKENS * (K * D_IN + K * RANK + RANK * D_IN)
 BYTES = 2 * (TOKENS * K + K * D_IN + K * RANK + RANK * D_IN) + 4 * TOKENS * D_IN
@@ -51,6 +54,7 @@ def tile_loralinear_t_kernel(tc, x, weight, bias, lora_left, lora_right, grad_ou
         r_raw = const.tile([P, D_IN], BF16)
         r32 = const.tile([P, D_IN], F32)
         ident = const.tile([P, P], F32)
+        warm = const.tile([P, HALF], BF16)
 
         state = {}
 
@@ -66,41 +70,50 @@ def tile_loralinear_t_kernel(tc, x, weight, bias, lora_left, lora_right, grad_ou
                 in_=src.rearrange("p t (c i) -> p c t i", i=4),
             )
 
+        def groups_of(c):
+            return GROUPS_FIRST if c == 0 else GROUPS
+
         def one_transpose(c, i):
             if c >= N_CHUNKS:
                 return
+            s, u = divmod(i, 2)
+            gi = [k for k, ab in enumerate(groups_of(c)) if ab[0] <= s < ab[1]][0]
+            a, b = groups_of(c)[gi]
             if i == 0:
                 grp = grp_pool.tile([P, CHUNK * 4], BF16, align_bytes=64)
                 codes = code_pool.tile([P, CHUNK], U32, align_bytes=64)
                 scales = code_pool.tile([P, CHUNK], U8, align_bytes=64)
                 state[c] = {"grp": grp, "codes": codes, "scales": scales}
-            if i % 4 == 0:
-                tr = psum.tile([P, 2, 2, P], F32, tag="bank")
+                if c == 0:
+                    nc.vector.memset(codes[:, P:].bitcast(I32), 0)
+                    nc.vector.memset(scales[:, P:].bitcast(I32), 0)
+            if s == a and u == 0:
+                tr = psum.tile([P, b - a, 2, P], F32, tag="bank")
                 state[c]["tr"] = tr
             tr = state[c]["tr"]
             words = g_raw[:, c, :].bitcast(F32)
-            nc.tensor.transpose(tr[:, (i % 4) // 2, i % 2, :], words[:, i * P : (i + 1) * P], ident[:])
-            if i % 4 == 3:
-                j = i // 4
-                dst = state[c]["grp"][:].bitcast(F32)[:, j * 512 : (j + 1) * 512]
-                dst = dst.rearrange("q (s p u) -> q s p u", s=2, u=2)
+            nc.tensor.transpose(tr[:, s - a, u, :], words[:, i * P : (i + 1) * P], ident[:])
+            if s == b - 1 and u == 1:
+                dst = state[c]["grp"][:].bitcast(F32)[:, a * 256 : b * 256]
+                dst = dst.rearrange("q (s p u) -> q s p u", s=b - a, u=2)
                 src = tr[:].rearrange("q s u p -> q s p u")
-                if j == 0:
+                if gi % 2 == 0:
                     nc.vector.tensor_copy(out=dst, in_=src)
                 else:
                     nc.scalar.copy(out=dst, in_=src)
 
-        def quantise(c, j):
+        def quantise(c, gi):
             if c >= N_CHUNKS:
                 return
             st = state[c]
+            a, b = groups_of(c)[gi]
             nc.vector.quantize_mx(
-                out=st["codes"][:, j * 256 : (j + 1) * 256].bitcast(E5X4),
-                scales=st["scales"][:, j * 256 : (j + 1) * 256],
-                in_=st["grp"][:, j * 1024 : (j + 1) * 1024],
+                out=st["codes"][:, a * P : b * P].bitcast(E5X4),
+                scales=st["scales"][:, a * P : b * P],
+                in_=st["grp"][:, a * P * 4 : b * P * 4],
             )
 
-        def make_t(c, cuts):
+        def make_t(c, lo, hi):
             if c >= N_CHUNKS:
                 return
             st = state[c]
@@ -114,10 +127,15 @@ def tile_loralinear_t_kernel(tc, x, weight, bias, lora_left, lora_right, grad_ou
                 start=True,
                 stop=True,
             )
-            t_sb = t_pool.tile([P, CHUNK], F32)
-            for a, b in zip(cuts[:-1], cuts[1:]):
-                nc.scalar.copy(out=t_sb[:, a:b], in_=tt[:, a:b])
-            st["t"] = t_sb
+            if lo == 0:
+                t_sb = t_pool.tile([P, CHUNK], F32)
+                st["t"] = t_sb
+            nc.scalar.copy(out=st["t"][:, lo:hi], in_=tt[:, lo:hi])
+
+        def dummies(n):
+            for k in range(n):
+                idle = psum.tile([P, HALF], F32, tag="bank")
+                nc.tensor.matmul(out=idle[:], lhsT=warm[:, :P], rhs=warm[:], start=True, stop=True)
 
         def main_pass(c, s, h):
             st = state[c]
@@ -158,6 +176,16 @@ def tile_loralinear_t_kernel(tc, x, weight, bias, lora_left, lora_right, grad_ou
             rows = o[c * CHUNK + s * P : c * CHUNK + (s + 1) * P, :]
             last = c == N_CHUNKS - 1 and s == S - 1
             cols = slice(h * HALF, (h + 1) * HALF)
+            if last and h == H - 1:
+                for q in range(HALF // P):
+                    part = slice(h * HALF + q * P, h * HALF + (q + 1) * P)
+                    piece = psum.tile([P, P], F32, tag="bank")
+                    nc.tensor.matmul(
+                        out=piece[:], lhsT=state[c]["t"][:, s * P : (s + 1) * P], rhs=r32[:, part], start=True, stop=True
+                    )
+                    nc.vector.tensor_tensor(out=o_sb[:, part], in0=piece[:], in1=o_sb[:, part], op=ADD)
+                    nc.sync.dma_start(out=rows[:, part], in_=o_sb[:, part])
+                return
             acc = product(c, s, h)
             nc.vector.tensor_tensor(out=o_sb[:, cols], in0=acc[:], in1=o_sb[:, cols], op=ADD)
             if last:
@@ -165,66 +193,90 @@ def tile_loralinear_t_kernel(tc, x, weight, bias, lora_left, lora_right, grad_ou
             elif h == H - 1:
                 nc.sync.dma_start(out=rows, in_=o_sb[:])
 
-        def plain_bunch(c, place):
+        def plain_bunch(c):
             for i in range(S * H):
+                second(c, i, low_pass)
                 one_transpose(c + 2, i)
-                place(c, i, low_pass)
                 if i == 5:
                     quantise(c + 2, 0)
             quantise(c + 2, 1)
 
+        def quantise_w(h):
+            nc.vector.quantize_mx(
+                out=w_codes[:, h * HALF : (h + 1) * HALF].bitcast(E4X4),
+                scales=w_scales[:, h * HALF : (h + 1) * HALF],
+                in_=w_grp[:, h * HALF : (h + 1) * HALF, :].rearrange("p n t -> p (n t)"),
+            )
+
         with tc.manual_schedule():
-            load_g(0, 0, 2)
-            load_g(0, 2, 4)
+            load_g(0, 0, 1)
             nc.sync.dma_start(
                 out=l_raw[:].rearrange("q (u e) r -> q u (e r)", u=2),
                 in_=lora_left.rearrange("(u q e) r -> q u (e r)", u=2, e=2),
             )
-            nc.sync.dma_start(out=r_raw[:], in_=lora_right)
+            nc.sync.dma_start(out=r_raw[:, :HALF], in_=lora_right[:, :HALF])
+            load_g(0, 1, S)
+            nc.sync.dma_start(out=r_raw[:, HALF:], in_=lora_right[:, HALF:])
             load_g(1, 0, S)
-            load_g(2, 0, S)
             w_view = weight.rearrange("(u q e) n -> u q (e n)", u=2, e=2)
             for u in range(2):
                 nc.sync.dma_start(
                     out=w_raw[:, 2 * u : 2 * u + 2, :].rearrange("q e n -> q (e n)"), in_=w_view[u]
                 )
-            for c in range(3, N_CHUNKS):
+            for c in range(2, N_CHUNKS):
                 load_g(c, 0, S)
 
+            nc.vector.memset(warm[:], 0.0)
             make_identity(nc, ident[:])
-            nc.gpsimd.tensor_scalar(out=r32[:], in0=r_raw[:], scalar1=2.0, scalar2=0.0, op0=MULT, op1=ADD)
+            for h in range(H):
+                cols = slice(h * HALF, (h + 1) * HALF)
+                nc.gpsimd.tensor_scalar(
+                    out=r32[:, cols], in0=r_raw[:, cols], scalar1=2.0, scalar2=0.0, op0=MULT, op1=ADD
+                )
 
-            for i in range(8):
-                one_transpose(0, i)
+            dummies(4)
+            one_transpose(0, 0)
+            one_transpose(0, 1)
+            dummies(2)
             regroup(l_grp[:], l_raw[:])
             quantise(0, 0)
             nc.vector.quantize_mx(
                 out=l_codes[:].bitcast(E4X4), scales=l_scales[:], in_=l_grp[:].rearrange("p r t -> p (r t)")
             )
+            make_t(0, 0, P)
+            for i in range(2, 8):
+                one_transpose(0, i)
             quantise(0, 1)
-            make_t(0, [0, P, CHUNK])
-            for i in range(8):
-                one_transpose(1, i)
-            quantise(1, 0)
-            quantise(1, 1)
-            for h in range(H):
-                regroup(w_grp[:, h * HALF : (h + 1) * HALF, :], w_raw[:, :, h * HALF : (h + 1) * HALF])
-            for h in range(H):
-                nc.vector.quantize_mx(
-                    out=w_codes[:, h * HALF : (h + 1) * HALF].bitcast(E4X4),
-                    scales=w_scales[:, h * HALF : (h + 1) * HALF],
-                    in_=w_grp[:, h * HALF : (h + 1) * HALF, :].rearrange("p n t -> p (n t)"),
-                )
+            quantise(0, 2)
 
-            plain_bunch(0, first)
-            make_t(1, [0, CHUNK])
+            for i in range(S * H):
+                first(0, i, low_pass)
+                if i == 0:
+                    make_t(0, P, CHUNK)
+                ahead = 1 if i < 4 else 2
+                one_transpose(ahead, 2 * (i % 4))
+                one_transpose(ahead, 2 * (i % 4) + 1)
+                if i == 2:
+                    quantise(1, 0)
+                if i == 4:
+                    quantise(1, 1)
+                    for h in range(H):
+                        regroup(w_grp[:, h * HALF : (h + 1) * HALF, :], w_raw[:, :, h * HALF : (h + 1) * HALF])
+                if i == 5:
+                    quantise_w(0)
+                    quantise_w(1)
+                if i == 7:
+                    quantise(2, 0)
+            quantise(2, 1)
+
+            make_t(1, 0, CHUNK)
             for i in range(S * H):
                 second(0, i, main_pass)
                 first(1, i, main_pass)
-            make_t(2, [0, CHUNK])
-            plain_bunch(1, second)
+            make_t(2, 0, CHUNK)
+            plain_bunch(1)
             for c in range(2, N_CHUNKS):
                 for i in range(S * H):
                     first(c, i, main_pass)
-                make_t(c + 1, [0, CHUNK])
-                plain_bunch(c, second)
+                make_t(c + 1, 0, CHUNK)
+                plain_bunch(c)

@@ -25,6 +25,7 @@ HALF = 512
 H = D_IN // HALF
 GROUPS_FIRST = [(0, 1), (1, 3), (3, 4)]
 GROUPS = [(0, 2), (2, 4)]
+FIRST_VECTOR_CHUNK = 3
 
 FLOPS = 2 * TOKENS * (K * D_IN + K * RANK + RANK * D_IN)
 BYTES = 2 * (TOKENS * K + K * D_IN + K * RANK + RANK * D_IN) + 4 * TOKENS * D_IN
@@ -42,7 +43,7 @@ def tile_loralinear_t_kernel(tc, x, weight, bias, lora_left, lora_right, grad_ou
         o_pool = ctx.enter_context(tc.tile_pool(name="o", bufs=10))
         psum = ctx.enter_context(tc.psum_pool(name="psum", bufs=8))
 
-        g_raw = const.tile([P, N_CHUNKS, S * K], BF16)
+        g_raw = const.tile([P, N_CHUNKS, S * K], BF16, align_bytes=64)
         w_raw = const.tile([P, 4, D_IN], BF16)
         w_grp = const.tile([P, D_IN, 4], BF16, align_bytes=64)
         w_codes = const.tile([P, D_IN], U32, align_bytes=64)
@@ -62,6 +63,28 @@ def tile_loralinear_t_kernel(tc, x, weight, bias, lora_left, lora_right, grad_ou
             nc.sync.dma_start(
                 out=g_raw[:, c, s0 * K : s1 * K].rearrange("p (s k) -> p s k", k=K),
                 in_=g[c * CHUNK + s0 * P : c * CHUNK + s1 * P, :].rearrange("(s p) k -> p s k", p=P),
+            )
+
+        g_rows = g.rearrange("t (u k) -> (t u) k", u=2)
+
+        def load_quadrant(c, q):
+            nc.sync.dma_start(
+                out=g_raw[32 * q : 32 * q + 32, c, :].rearrange("i (b k) -> i b k", k=64),
+                in_=g_rows[c * 2 * CHUNK : (c + 1) * 2 * CHUNK, 64 * q : 64 * q + 64].rearrange("(b i) k -> i b k", i=32),
+            )
+
+        def vector_transpose(c, gi):
+            if c >= N_CHUNKS:
+                return
+            if gi == 0:
+                grp = grp_pool.tile([P, CHUNK * 4], BF16, align_bytes=64)
+                codes = code_pool.tile([P, CHUNK], U32, align_bytes=64)
+                scales = code_pool.tile([P, CHUNK], U8, align_bytes=64)
+                state[c] = {"grp": grp, "codes": codes, "scales": scales}
+            a, b = GROUPS[gi]
+            nc.vector.transpose(
+                out=state[c]["grp"][:, a * P * 4 : b * P * 4].bitcast(F32),
+                in_=g_raw[:, c, a * P * 4 : b * P * 4].bitcast(F32),
             )
 
         def regroup(dst, src):
@@ -192,11 +215,17 @@ def tile_loralinear_t_kernel(tc, x, weight, bias, lora_left, lora_right, grad_ou
                 nc.sync.dma_start(out=rows[:, cols], in_=o_sb[:, cols])
             elif h == H - 1:
                 nc.sync.dma_start(out=rows, in_=o_sb[:])
+                later, q = divmod(c * S + s, 4)
+                if FIRST_VECTOR_CHUNK + 1 + later < N_CHUNKS:
+                    load_quadrant(FIRST_VECTOR_CHUNK + 1 + later, q)
 
         def plain_bunch(c):
             for i in range(S * H):
                 second(c, i, low_pass)
-                one_transpose(c + 2, i)
+                if i == 1:
+                    vector_transpose(c + 2, 0)
+                if i == 3:
+                    vector_transpose(c + 2, 1)
                 if i == 5:
                     quantise(c + 2, 0)
             quantise(c + 2, 1)
@@ -223,8 +252,9 @@ def tile_loralinear_t_kernel(tc, x, weight, bias, lora_left, lora_right, grad_ou
                 nc.sync.dma_start(
                     out=w_raw[:, 2 * u : 2 * u + 2, :].rearrange("q e n -> q (e n)"), in_=w_view[u]
                 )
-            for c in range(2, N_CHUNKS):
-                load_g(c, 0, S)
+            load_g(2, 0, S)
+            for q in range(4):
+                load_quadrant(FIRST_VECTOR_CHUNK, q)
 
             nc.vector.memset(warm[:], 0.0)
             make_identity(nc, ident[:])

@@ -38,9 +38,9 @@ def tile_loralinear_t_kernel(tc, x, weight, bias, lora_left, lora_right, grad_ou
     with ExitStack() as ctx:
         const = ctx.enter_context(tc.tile_pool(name="const", bufs=1))
         grp_pool = ctx.enter_context(tc.tile_pool(name="grp", bufs=2))
-        code_pool = ctx.enter_context(tc.tile_pool(name="codes", bufs=3))
+        code_pool = ctx.enter_context(tc.tile_pool(name="codes", bufs=4))
         t_pool = ctx.enter_context(tc.tile_pool(name="tT", bufs=2))
-        o_pool = ctx.enter_context(tc.tile_pool(name="o", bufs=10))
+        o_pool = ctx.enter_context(tc.tile_pool(name="o", bufs=12))
         psum = ctx.enter_context(tc.psum_pool(name="psum", bufs=8))
 
         g_raw = const.tile([P, N_CHUNKS, S * K], BF16, align_bytes=64)
@@ -215,20 +215,9 @@ def tile_loralinear_t_kernel(tc, x, weight, bias, lora_left, lora_right, grad_ou
                 nc.sync.dma_start(out=rows[:, cols], in_=o_sb[:, cols])
             elif h == H - 1:
                 nc.sync.dma_start(out=rows, in_=o_sb[:])
-                later, q = divmod(c * S + s, 4)
-                if FIRST_VECTOR_CHUNK + 1 + later < N_CHUNKS:
-                    load_quadrant(FIRST_VECTOR_CHUNK + 1 + later, q)
-
-        def plain_bunch(c):
-            for i in range(S * H):
-                second(c, i, low_pass)
-                if i == 1:
-                    vector_transpose(c + 2, 0)
-                if i == 3:
-                    vector_transpose(c + 2, 1)
-                if i == 5:
-                    quantise(c + 2, 0)
-            quantise(c + 2, 1)
+                later = 5 if c == 0 else c + 4
+                if c != 1 and later < N_CHUNKS:
+                    load_quadrant(later, s)
 
         def quantise_w(h):
             nc.vector.quantize_mx(
@@ -253,8 +242,9 @@ def tile_loralinear_t_kernel(tc, x, weight, bias, lora_left, lora_right, grad_ou
                     out=w_raw[:, 2 * u : 2 * u + 2, :].rearrange("q e n -> q (e n)"), in_=w_view[u]
                 )
             load_g(2, 0, S)
-            for q in range(4):
-                load_quadrant(FIRST_VECTOR_CHUNK, q)
+            for c in (FIRST_VECTOR_CHUNK, FIRST_VECTOR_CHUNK + 1):
+                for q in range(4):
+                    load_quadrant(c, q)
 
             nc.vector.memset(warm[:], 0.0)
             make_identity(nc, ident[:])
@@ -295,18 +285,24 @@ def tile_loralinear_t_kernel(tc, x, weight, bias, lora_left, lora_right, grad_ou
                 if i == 5:
                     quantise_w(0)
                     quantise_w(1)
+                if i == 6:
+                    make_t(1, 0, CHUNK)
                 if i == 7:
                     quantise(2, 0)
             quantise(2, 1)
 
-            make_t(1, 0, CHUNK)
-            for i in range(S * H):
-                second(0, i, main_pass)
-                first(1, i, main_pass)
-            make_t(2, 0, CHUNK)
-            plain_bunch(1)
-            for c in range(2, N_CHUNKS):
+            for c in range(1, N_CHUNKS):
                 for i in range(S * H):
+                    if c == 1:
+                        second(0, i, main_pass)
                     first(c, i, main_pass)
-                make_t(c + 1, 0, CHUNK)
-                plain_bunch(c)
+                    second(c, i, low_pass)
+                    if i == 2:
+                        vector_transpose(c + 2, 0)
+                    if i == 3:
+                        make_t(c + 1, 0, CHUNK)
+                    if i == 4:
+                        vector_transpose(c + 2, 1)
+                    if i == 6:
+                        quantise(c + 2, 0)
+                quantise(c + 2, 1)

@@ -12,6 +12,7 @@ E4X4 = mybir.dt.float8_e4m3fn_x4
 E5X4 = mybir.dt.float8_e5m2_x4
 ADD = mybir.AluOpType.add
 MULT = mybir.AluOpType.mult
+SUBTRACT = mybir.AluOpType.subtract
 
 P = 128
 TOKENS = 4096
@@ -25,6 +26,8 @@ HALF = 512
 H = D_IN // HALF
 GROUPS_FIRST = [(0, 1), (1, 3), (3, 4)]
 GROUPS = [(0, 2), (2, 4)]
+SPLIT_CHUNKS = (2, 3, 4, 5)
+SPLIT_TILE = S - 1
 FIRST_VECTOR_CHUNK = 3
 
 FLOPS = 2 * TOKENS * (K * D_IN + K * RANK + RANK * D_IN)
@@ -40,6 +43,7 @@ def tile_loralinear_t_kernel(tc, x, weight, bias, lora_left, lora_right, grad_ou
         grp_pool = ctx.enter_context(tc.tile_pool(name="grp", bufs=2))
         code_pool = ctx.enter_context(tc.tile_pool(name="codes", bufs=4))
         t_pool = ctx.enter_context(tc.tile_pool(name="tT", bufs=2))
+        split_pool = ctx.enter_context(tc.tile_pool(name="split", bufs=2))
         o_pool = ctx.enter_context(tc.tile_pool(name="o", bufs=12))
         psum = ctx.enter_context(tc.psum_pool(name="psum", bufs=8))
 
@@ -54,6 +58,7 @@ def tile_loralinear_t_kernel(tc, x, weight, bias, lora_left, lora_right, grad_ou
         l_scales = const.tile([P, RANK], U8, align_bytes=64)
         r_raw = const.tile([P, D_IN], BF16)
         r32 = const.tile([P, D_IN], F32)
+        r16 = const.tile([P, D_IN], BF16)
         ident = const.tile([P, P], F32)
         warm = const.tile([P, HALF], BF16)
 
@@ -185,6 +190,38 @@ def tile_loralinear_t_kernel(tc, x, weight, bias, lora_left, lora_right, grad_ou
             )
             return acc
 
+        def split(c, step):
+            if c not in SPLIT_CHUNKS:
+                return
+            st = state[c]
+            t_cols = st["t"][:, SPLIT_TILE * P : (SPLIT_TILE + 1) * P]
+            if step == 0:
+                parts = split_pool.tile([P, 3, P], BF16)
+                rest = split_pool.tile([P, P], F32)
+                st["parts"] = parts
+                st["rest"] = rest
+                nc.vector.tensor_copy(out=parts[:, 0, :], in_=t_cols)
+            if step == 1:
+                nc.vector.tensor_tensor(out=st["rest"][:], in0=t_cols, in1=st["parts"][:, 0, :], op=SUBTRACT)
+            if step == 2:
+                nc.vector.tensor_copy(out=st["parts"][:, 1, :], in_=st["rest"][:])
+            if step == 3:
+                nc.vector.tensor_tensor(out=st["parts"][:, 2, :], in0=st["rest"][:], in1=st["parts"][:, 1, :], op=SUBTRACT)
+
+        def low_pass_any(c, s, h):
+            if c not in SPLIT_CHUNKS or s != SPLIT_TILE:
+                return low_pass(c, s, h)
+            acc = psum.tile([P, HALF], F32, tag="bank")
+            for j in range(3):
+                nc.tensor.matmul(
+                    out=acc[:],
+                    lhsT=state[c]["parts"][:, j, :],
+                    rhs=r16[:, h * HALF : (h + 1) * HALF],
+                    start=(j == 0),
+                    stop=(j == 2),
+                )
+            return acc
+
         def first(c, i, product):
             s, h = divmod(i, H)
             if h == 0:
@@ -253,8 +290,9 @@ def tile_loralinear_t_kernel(tc, x, weight, bias, lora_left, lora_right, grad_ou
                 nc.gpsimd.tensor_scalar(
                     out=r32[:, cols], in0=r_raw[:, cols], scalar1=2.0, scalar2=0.0, op0=MULT, op1=ADD
                 )
+            nc.gpsimd.tensor_scalar(out=r16[:], in0=r_raw[:], scalar1=2.0, scalar2=0.0, op0=MULT, op1=ADD)
 
-            dummies(4)
+            dummies(2)
             one_transpose(0, 0)
             one_transpose(0, 1)
             dummies(2)
@@ -296,7 +334,8 @@ def tile_loralinear_t_kernel(tc, x, weight, bias, lora_left, lora_right, grad_ou
                     if c == 1:
                         second(0, i, main_pass)
                     first(c, i, main_pass)
-                    second(c, i, low_pass)
+                    second(c, i, low_pass_any)
+                    split(c, i)
                     if i == 2:
                         vector_transpose(c + 2, 0)
                     if i == 3:

@@ -13,6 +13,7 @@ E5X4 = mybir.dt.float8_e5m2_x4
 ADD = mybir.AluOpType.add
 MULT = mybir.AluOpType.mult
 SUBTRACT = mybir.AluOpType.subtract
+COPY = mybir.ActivationFunctionType.Copy
 
 P = 128
 TOKENS = 4096
@@ -72,21 +73,29 @@ def tile_loralinear_t_kernel(tc, x, weight, bias, lora_left, lora_right, grad_ou
 
         g_rows = g.rearrange("t (u k) -> (t u) k", u=2)
 
-        def load_quadrant(c, q):
+        def load_quadrant(c, q, b0=0, b1=CHUNK // 16):
             nc.sync.dma_start(
-                out=g_raw[32 * q : 32 * q + 32, c, :].rearrange("i (b k) -> i b k", k=64),
-                in_=g_rows[c * 2 * CHUNK : (c + 1) * 2 * CHUNK, 64 * q : 64 * q + 64].rearrange("(b i) k -> i b k", i=32),
+                out=g_raw[32 * q : 32 * q + 32, c, 64 * b0 : 64 * b1].rearrange("i (b k) -> i b k", k=64),
+                in_=g_rows[c * 2 * CHUNK + 32 * b0 : c * 2 * CHUNK + 32 * b1, 64 * q : 64 * q + 64].rearrange(
+                    "(b i) k -> i b k", i=32
+                ),
             )
+
+        def open_chunk(c):
+            grp = grp_pool.tile([P, CHUNK * 4], BF16, align_bytes=64)
+            codes = code_pool.tile([P, CHUNK], U32, align_bytes=64)
+            scales = code_pool.tile([P, CHUNK], U8, align_bytes=64)
+            state[c] = {"grp": grp, "codes": codes, "scales": scales}
+            if c == 0:
+                nc.vector.memset(codes[:, P:].bitcast(I32), 0)
+                nc.vector.memset(scales[:, P:].bitcast(I32), 0)
 
         def vector_transpose(c, gi):
             if c >= N_CHUNKS:
                 return
             if gi == 0:
-                grp = grp_pool.tile([P, CHUNK * 4], BF16, align_bytes=64)
-                codes = code_pool.tile([P, CHUNK], U32, align_bytes=64)
-                scales = code_pool.tile([P, CHUNK], U8, align_bytes=64)
-                state[c] = {"grp": grp, "codes": codes, "scales": scales}
-            a, b = GROUPS[gi]
+                open_chunk(c)
+            a, b = groups_of(c)[gi]
             nc.vector.transpose(
                 out=state[c]["grp"][:, a * P * 4 : b * P * 4].bitcast(F32),
                 in_=g_raw[:, c, a * P * 4 : b * P * 4].bitcast(F32),
@@ -108,13 +117,7 @@ def tile_loralinear_t_kernel(tc, x, weight, bias, lora_left, lora_right, grad_ou
             gi = [k for k, ab in enumerate(groups_of(c)) if ab[0] <= s < ab[1]][0]
             a, b = groups_of(c)[gi]
             if i == 0:
-                grp = grp_pool.tile([P, CHUNK * 4], BF16, align_bytes=64)
-                codes = code_pool.tile([P, CHUNK], U32, align_bytes=64)
-                scales = code_pool.tile([P, CHUNK], U8, align_bytes=64)
-                state[c] = {"grp": grp, "codes": codes, "scales": scales}
-                if c == 0:
-                    nc.vector.memset(codes[:, P:].bitcast(I32), 0)
-                    nc.vector.memset(scales[:, P:].bitcast(I32), 0)
+                open_chunk(c)
             if s == a and u == 0:
                 tr = psum.tile([P, b - a, 2, P], F32, tag="bank")
                 state[c]["tr"] = tr
@@ -125,7 +128,7 @@ def tile_loralinear_t_kernel(tc, x, weight, bias, lora_left, lora_right, grad_ou
                 dst = state[c]["grp"][:].bitcast(F32)[:, a * 256 : b * 256]
                 dst = dst.rearrange("q (s p u) -> q s p u", s=b - a, u=2)
                 src = tr[:].rearrange("q s u p -> q s p u")
-                if gi % 2 == 0:
+                if (gi + (1 if c == 0 else 0)) % 2 == 0:
                     nc.vector.tensor_copy(out=dst, in_=src)
                 else:
                     nc.scalar.copy(out=dst, in_=src)
@@ -264,20 +267,20 @@ def tile_loralinear_t_kernel(tc, x, weight, bias, lora_left, lora_right, grad_ou
             )
 
         with tc.manual_schedule():
-            load_g(0, 0, 1)
+            for q in range(4):
+                load_quadrant(0, q, 0, P // 16)
             nc.sync.dma_start(
                 out=l_raw[:].rearrange("q (u e) r -> q u (e r)", u=2),
                 in_=lora_left.rearrange("(u q e) r -> q u (e r)", u=2, e=2),
             )
             nc.sync.dma_start(out=r_raw[:, :HALF], in_=lora_right[:, :HALF])
             load_g(0, 1, S)
-            nc.sync.dma_start(out=r_raw[:, HALF:], in_=lora_right[:, HALF:])
             load_g(1, 0, S)
-            w_view = weight.rearrange("(u q e) n -> u q (e n)", u=2, e=2)
-            for u in range(2):
-                nc.sync.dma_start(
-                    out=w_raw[:, 2 * u : 2 * u + 2, :].rearrange("q e n -> q (e n)"), in_=w_view[u]
-                )
+            nc.sync.dma_start(out=r_raw[:, HALF:], in_=lora_right[:, HALF:])
+            nc.sync.dma_start(
+                out=w_raw[:].rearrange("q (u e) n -> q u (e n)", u=2),
+                in_=weight.rearrange("(u q e) n -> q u (e n)", u=2, e=2),
+            )
             load_g(2, 0, S)
             for c in (FIRST_VECTOR_CHUNK, FIRST_VECTOR_CHUNK + 1):
                 for q in range(4):
@@ -285,17 +288,14 @@ def tile_loralinear_t_kernel(tc, x, weight, bias, lora_left, lora_right, grad_ou
 
             nc.vector.memset(warm[:], 0.0)
             make_identity(nc, ident[:])
-            for h in range(H):
-                cols = slice(h * HALF, (h + 1) * HALF)
-                nc.gpsimd.tensor_scalar(
-                    out=r32[:, cols], in0=r_raw[:, cols], scalar1=2.0, scalar2=0.0, op0=MULT, op1=ADD
-                )
+            nc.scalar.activation(out=r32[:, :HALF], in_=r_raw[:, :HALF], func=COPY, scale=2.0)
+            nc.gpsimd.tensor_scalar(
+                out=r32[:, HALF:], in0=r_raw[:, HALF:], scalar1=2.0, scalar2=0.0, op0=MULT, op1=ADD
+            )
             nc.gpsimd.tensor_scalar(out=r16[:], in0=r_raw[:], scalar1=2.0, scalar2=0.0, op0=MULT, op1=ADD)
 
-            dummies(2)
-            one_transpose(0, 0)
-            one_transpose(0, 1)
-            dummies(2)
+            dummies(4)
+            vector_transpose(0, 0)
             regroup(l_grp[:], l_raw[:])
             quantise(0, 0)
             nc.vector.quantize_mx(

@@ -27,7 +27,7 @@ HALF = 512
 H = D_IN // HALF
 GROUPS_FIRST = [(0, 1), (1, 3), (3, 4)]
 GROUPS = [(0, 2), (2, 4)]
-SPLIT_CHUNKS = (2, 3, 4, 5)
+SPLIT_CHUNKS = (2, 3, 4, 5, 6)
 SPLIT_TILE = S - 1
 FIRST_VECTOR_CHUNK = 3
 
@@ -61,7 +61,6 @@ def tile_loralinear_t_kernel(tc, x, weight, bias, lora_left, lora_right, grad_ou
         r32 = const.tile([P, D_IN], F32)
         r16 = const.tile([P, D_IN], BF16)
         ident = const.tile([P, P], F32)
-        warm = const.tile([P, HALF], BF16)
 
         state = {}
 
@@ -162,11 +161,6 @@ def tile_loralinear_t_kernel(tc, x, weight, bias, lora_left, lora_right, grad_ou
                 t_sb = t_pool.tile([P, CHUNK], F32)
                 st["t"] = t_sb
             nc.scalar.copy(out=st["t"][:, lo:hi], in_=tt[:, lo:hi])
-
-        def dummies(n):
-            for k in range(n):
-                idle = psum.tile([P, HALF], F32, tag="bank")
-                nc.tensor.matmul(out=idle[:], lhsT=warm[:, :P], rhs=warm[:], start=True, stop=True)
 
         def main_pass(c, s, h):
             st = state[c]
@@ -286,7 +280,6 @@ def tile_loralinear_t_kernel(tc, x, weight, bias, lora_left, lora_right, grad_ou
                 for q in range(4):
                     load_quadrant(c, q)
 
-            nc.vector.memset(warm[:], 0.0)
             make_identity(nc, ident[:])
             nc.scalar.activation(out=r32[:, :HALF], in_=r_raw[:, :HALF], func=COPY, scale=2.0)
             nc.gpsimd.tensor_scalar(
@@ -294,7 +287,6 @@ def tile_loralinear_t_kernel(tc, x, weight, bias, lora_left, lora_right, grad_ou
             )
             nc.gpsimd.tensor_scalar(out=r16[:], in0=r_raw[:], scalar1=2.0, scalar2=0.0, op0=MULT, op1=ADD)
 
-            dummies(4)
             vector_transpose(0, 0)
             regroup(l_grp[:], l_raw[:])
             quantise(0, 0)

@@ -48,15 +48,15 @@ def tile_loralinear_t_kernel(tc, x, weight, bias, lora_left, lora_right, grad_ou
         o_pool = ctx.enter_context(tc.tile_pool(name="o", bufs=12))
         psum = ctx.enter_context(tc.psum_pool(name="psum", bufs=8))
 
-        g_raw = const.tile([P, N_CHUNKS, S * K], BF16, align_bytes=64)
+        g_raw = const.tile([P, N_CHUNKS, S * K], BF16, align_bytes=256)
         w_raw = const.tile([P, 4, D_IN], BF16)
-        w_grp = const.tile([P, D_IN, 4], BF16, align_bytes=64)
-        w_codes = const.tile([P, D_IN], U32, align_bytes=64)
-        w_scales = const.tile([P, D_IN], U8, align_bytes=64)
+        w_grp = const.tile([P, D_IN, 4], BF16, align_bytes=256)
+        w_codes = const.tile([P, D_IN], U32, align_bytes=256)
+        w_scales = const.tile([P, D_IN], U8, align_bytes=256)
         l_raw = const.tile([P, 4, RANK], BF16)
-        l_grp = const.tile([P, RANK, 4], BF16, align_bytes=64)
-        l_codes = const.tile([P, RANK], U32, align_bytes=64)
-        l_scales = const.tile([P, RANK], U8, align_bytes=64)
+        l_grp = const.tile([P, RANK, 4], BF16, align_bytes=256)
+        l_codes = const.tile([P, RANK], U32, align_bytes=256)
+        l_scales = const.tile([P, RANK], U8, align_bytes=256)
         r_raw = const.tile([P, D_IN], BF16)
         r32 = const.tile([P, D_IN], F32)
         r16 = const.tile([P, D_IN], BF16)
@@ -81,9 +81,9 @@ def tile_loralinear_t_kernel(tc, x, weight, bias, lora_left, lora_right, grad_ou
             )
 
         def open_chunk(c):
-            grp = grp_pool.tile([P, CHUNK * 4], BF16, align_bytes=64)
-            codes = code_pool.tile([P, CHUNK], U32, align_bytes=64)
-            scales = code_pool.tile([P, CHUNK], U8, align_bytes=64)
+            grp = grp_pool.tile([P, CHUNK * 4], BF16, align_bytes=256)
+            codes = code_pool.tile([P, CHUNK], U32, align_bytes=256)
+            scales = code_pool.tile([P, CHUNK], U8, align_bytes=256)
             state[c] = {"grp": grp, "codes": codes, "scales": scales}
             if c == 0:
                 nc.vector.memset(codes[:, P:].bitcast(I32), 0)

from contextlib import ExitStack

import concourse.mybir as mybir
from concourse.masks import make_identity

F32 = mybir.dt.float32
BF16 = mybir.dt.bfloat16
U32 = mybir.dt.uint32
U8 = mybir.dt.uint8
I32 = mybir.dt.int32
E4X4 = mybir.dt.float8_e4m3fn_x4
E5X4 = mybir.dt.float8_e5m2_x4
ADD = mybir.AluOpType.add
MULT = mybir.AluOpType.mult
SUBTRACT = mybir.AluOpType.subtract
COPY = mybir.ActivationFunctionType.Copy

P = 128
TOKENS = 4096
K = 512
D_IN = 1024
RANK = 128
CHUNK = 512
N_CHUNKS = TOKENS // CHUNK
S = CHUNK // P
HALF = 512
H = D_IN // HALF
GROUPS_FIRST = [(0, 1), (1, 3), (3, 4)]
GROUPS = [(0, 2), (2, 4)]
SPLIT_CHUNKS = (2, 3, 4, 5, 6)
SPLIT_TILE = S - 1
FIRST_VECTOR_CHUNK = 3

FLOPS = 2 * TOKENS * (K * D_IN + K * RANK + RANK * D_IN)
BYTES = 2 * (TOKENS * K + K * D_IN + K * RANK + RANK * D_IN) + 4 * TOKENS * D_IN


def tile_loralinear_t_kernel(tc, x, weight, bias, lora_left, lora_right, grad_out, out):
    nc = tc.nc
    g = grad_out.flatten_outer_dims()
    o = out.flatten_outer_dims()
    with ExitStack() as ctx:
        const = ctx.enter_context(tc.tile_pool(name="const", bufs=1))
        grp_pool = ctx.enter_context(tc.tile_pool(name="grp", bufs=2))
        code_pool = ctx.enter_context(tc.tile_pool(name="codes", bufs=4))
        t_pool = ctx.enter_context(tc.tile_pool(name="tT", bufs=2))
        split_pool = ctx.enter_context(tc.tile_pool(name="split", bufs=2))
        o_pool = ctx.enter_context(tc.tile_pool(name="o", bufs=12))
        psum = ctx.enter_context(tc.psum_pool(name="psum", bufs=8))

        g_raw = const.tile([P, N_CHUNKS, S * K], BF16, align_bytes=256)
        w_raw = const.tile([P, 4, D_IN], BF16)
        w_grp = const.tile([P, D_IN, 4], BF16, align_bytes=256)
        w_codes = const.tile([P, D_IN], U32, align_bytes=256)
        w_scales = const.tile([P, D_IN], U8, align_bytes=256)
        l_raw = const.tile([P, 4, RANK], BF16)
        l_grp = const.tile([P, RANK, 4], BF16, align_bytes=256)
        l_codes = const.tile([P, RANK], U32, align_bytes=256)
        l_scales = const.tile([P, RANK], U8, align_bytes=256)
        r_raw = const.tile([P, D_IN], BF16)
        r32 = const.tile([P, D_IN], F32)
        r16 = const.tile([P, D_IN], BF16)
        ident = const.tile([P, P], F32)

        state = {}

        def load_g(c, s0, s1):
            nc.sync.dma_start(
                out=g_raw[:, c, s0 * K : s1 * K].rearrange("p (s k) -> p s k", k=K),
                in_=g[c * CHUNK + s0 * P : c * CHUNK + s1 * P, :].rearrange("(s p) k -> p s k", p=P),
            )

        g_rows = g.rearrange("t (u k) -> (t u) k", u=2)

        def load_quadrant(c, q, b0=0, b1=CHUNK // 16):
            nc.sync.dma_start(
                out=g_raw[32 * q : 32 * q + 32, c, 64 * b0 : 64 * b1].rearrange("i (b k) -> i b k", k=64),
                in_=g_rows[c * 2 * CHUNK + 32 * b0 : c * 2 * CHUNK + 32 * b1, 64 * q : 64 * q + 64].rearrange(
                    "(b i) k -> i b k", i=32
                ),
            )

        def open_chunk(c):
            grp = grp_pool.tile([P, CHUNK * 4], BF16, align_bytes=256)
            codes = code_pool.tile([P, CHUNK], U32, align_bytes=256)
            scales = code_pool.tile([P, CHUNK], U8, align_bytes=256)
            state[c] = {"grp": grp, "codes": codes, "scales": scales}
            if c == 0:
                nc.vector.memset(codes[:, P:].bitcast(I32), 0)
                nc.vector.memset(scales[:, P:].bitcast(I32), 0)

        def vector_transpose(c, gi):
            if c >= N_CHUNKS:
                return
            if gi == 0:
                open_chunk(c)
            a, b = groups_of(c)[gi]
            nc.vector.transpose(
                out=state[c]["grp"][:, a * P * 4 : b * P * 4].bitcast(F32),
                in_=g_raw[:, c, a * P * 4 : b * P * 4].bitcast(F32),
            )

        def regroup(dst, src):
            nc.vector.tensor_copy(
                out=dst.rearrange("p (c i) t -> p c t i", i=4),
                in_=src.rearrange("p t (c i) -> p c t i", i=4),
            )

        def groups_of(c):
            return GROUPS_FIRST if c == 0 else GROUPS

        def one_transpose(c, i):
            if c >= N_CHUNKS:
                return
            s, u = divmod(i, 2)
            gi = [k for k, ab in enumerate(groups_of(c)) if ab[0] <= s < ab[1]][0]
            a, b = groups_of(c)[gi]
            if i == 0:
                open_chunk(c)
            if s == a and u == 0:
                tr = psum.tile([P, b - a, 2, P], F32, tag="bank")
                state[c]["tr"] = tr
            tr = state[c]["tr"]
            words = g_raw[:, c, :].bitcast(F32)
            nc.tensor.transpose(tr[:, s - a, u, :], words[:, i * P : (i + 1) * P], ident[:])
            if s == b - 1 and u == 1:
                dst = state[c]["grp"][:].bitcast(F32)[:, a * 256 : b * 256]
                dst = dst.rearrange("q (s p u) -> q s p u", s=b - a, u=2)
                src = tr[:].rearrange("q s u p -> q s p u")
                if (gi + (1 if c == 0 else 0)) % 2 == 0:
                    nc.vector.tensor_copy(out=dst, in_=src)
                else:
                    nc.scalar.copy(out=dst, in_=src)

        def quantise(c, gi):
            if c >= N_CHUNKS:
                return
            st = state[c]
            a, b = groups_of(c)[gi]
            nc.vector.quantize_mx(
                out=st["codes"][:, a * P : b * P].bitcast(E5X4),
                scales=st["scales"][:, a * P : b * P],
                in_=st["grp"][:, a * P * 4 : b * P * 4],
            )

        def make_t(c, lo, hi):
            if c >= N_CHUNKS:
                return
            st = state[c]
            tt = psum.tile([P, CHUNK], F32, tag="bank")
            nc.tensor.matmul_mx(
                out=tt[:],
                lhsT=l_codes[:].bitcast(E4X4),
                lhsT_scale=l_scales[:],
                rhs=st["codes"][:].bitcast(E5X4),
                rhs_scale=st["scales"][:],
                start=True,
                stop=True,
            )
            if lo == 0:
                t_sb = t_pool.tile([P, CHUNK], F32)
                st["t"] = t_sb
            nc.scalar.copy(out=st["t"][:, lo:hi], in_=tt[:, lo:hi])

        def main_pass(c, s, h):
            st = state[c]
            acc = psum.tile([P, HALF], F32, tag="bank")
            nc.tensor.matmul_mx(
                out=acc[:],
                lhsT=st["codes"][:, s * P : (s + 1) * P].bitcast(E5X4),
                lhsT_scale=st["scales"][:, s * P : (s + 1) * P],
                rhs=w_codes[:, h * HALF : (h + 1) * HALF].bitcast(E4X4),
                rhs_scale=w_scales[:, h * HALF : (h + 1) * HALF],
                start=True,
                stop=True,
            )
            return acc

        def low_pass(c, s, h):
            acc = psum.tile([P, HALF], F32, tag="bank")
            nc.tensor.matmul(
                out=acc[:],
                lhsT=state[c]["t"][:, s * P : (s + 1) * P],
                rhs=r32[:, h * HALF : (h + 1) * HALF],
                start=True,
                stop=True,
            )
            return acc

        def split(c, step):
            if c not in SPLIT_CHUNKS:
                return
            st = state[c]
            t_cols = st["t"][:, SPLIT_TILE * P : (SPLIT_TILE + 1) * P]
            if step == 0:
                parts = split_pool.tile([P, 3, P], BF16)
                rest = split_pool.tile([P, P], F32)
                st["parts"] = parts
                st["rest"] = rest
                nc.vector.tensor_copy(out=parts[:, 0, :], in_=t_cols)
            if step == 1:
                nc.vector.tensor_tensor(out=st["rest"][:], in0=t_cols, in1=st["parts"][:, 0, :], op=SUBTRACT)
            if step == 2:
                nc.vector.tensor_copy(out=st["parts"][:, 1, :], in_=st["rest"][:])
            if step == 3:
                nc.vector.tensor_tensor(out=st["parts"][:, 2, :], in0=st["rest"][:], in1=st["parts"][:, 1, :], op=SUBTRACT)

        def low_pass_any(c, s, h):
            if c not in SPLIT_CHUNKS or s != SPLIT_TILE:
                return low_pass(c, s, h)
            acc = psum.tile([P, HALF], F32, tag="bank")
            for j in range(3):
                nc.tensor.matmul(
                    out=acc[:],
                    lhsT=state[c]["parts"][:, j, :],
                    rhs=r16[:, h * HALF : (h + 1) * HALF],
                    start=(j == 0),
                    stop=(j == 2),
                )
            return acc

        def first(c, i, product):
            s, h = divmod(i, H)
            if h == 0:
                o_sb = o_pool.tile([P, D_IN], F32)
                state[(c, s)] = o_sb
            acc = product(c, s, h)
            nc.scalar.copy(out=state[(c, s)][:, h * HALF : (h + 1) * HALF], in_=acc[:])

        def second(c, i, product):
            s, h = divmod(i, H)
            o_sb = state[(c, s)]
            rows = o[c * CHUNK + s * P : c * CHUNK + (s + 1) * P, :]
            last = c == N_CHUNKS - 1 and s == S - 1
            cols = slice(h * HALF, (h + 1) * HALF)
            if last and h == H - 1:
                for q in range(HALF // P):
                    part = slice(h * HALF + q * P, h * HALF + (q + 1) * P)
                    piece = psum.tile([P, P], F32, tag="bank")
                    nc.tensor.matmul(
                        out=piece[:], lhsT=state[c]["t"][:, s * P : (s + 1) * P], rhs=r32[:, part], start=True, stop=True
                    )
                    nc.vector.tensor_tensor(out=o_sb[:, part], in0=piece[:], in1=o_sb[:, part], op=ADD)
                    nc.sync.dma_start(out=rows[:, part], in_=o_sb[:, part])
                return
            acc = product(c, s, h)
            nc.vector.tensor_tensor(out=o_sb[:, cols], in0=acc[:], in1=o_sb[:, cols], op=ADD)
            if last:
                nc.sync.dma_start(out=rows[:, cols], in_=o_sb[:, cols])
            elif h == H - 1:
                nc.sync.dma_start(out=rows, in_=o_sb[:])
                later = 5 if c == 0 else c + 4
                if c != 1 and later < N_CHUNKS:
                    load_quadrant(later, s)

        def quantise_w(h):
            nc.vector.quantize_mx(
                out=w_codes[:, h * HALF : (h + 1) * HALF].bitcast(E4X4),
                scales=w_scales[:, h * HALF : (h + 1) * HALF],
                in_=w_grp[:, h * HALF : (h + 1) * HALF, :].rearrange("p n t -> p (n t)"),
            )

        with tc.manual_schedule():
            for q in range(4):
                load_quadrant(0, q, 0, P // 16)
            nc.sync.dma_start(
                out=l_raw[:].rearrange("q (u e) r -> q u (e r)", u=2),
                in_=lora_left.rearrange("(u q e) r -> q u (e r)", u=2, e=2),
            )
            nc.sync.dma_start(out=r_raw[:, :HALF], in_=lora_right[:, :HALF])
            load_g(0, 1, S)
            load_g(1, 0, S)
            nc.sync.dma_start(out=r_raw[:, HALF:], in_=lora_right[:, HALF:])
            nc.sync.dma_start(
                out=w_raw[:].rearrange("q (u e) n -> q u (e n)", u=2),
                in_=weight.rearrange("(u q e) n -> q u (e n)", u=2, e=2),
            )
            load_g(2, 0, S)
            for c in (FIRST_VECTOR_CHUNK, FIRST_VECTOR_CHUNK + 1):
                for q in range(4):
                    load_quadrant(c, q)

            make_identity(nc, ident[:])
            nc.scalar.activation(out=r32[:, :HALF], in_=r_raw[:, :HALF], func=COPY, scale=2.0)
            nc.gpsimd.tensor_scalar(
                out=r32[:, HALF:], in0=r_raw[:, HALF:], scalar1=2.0, scalar2=0.0, op0=MULT, op1=ADD
            )
            nc.gpsimd.tensor_scalar(out=r16[:], in0=r_raw[:], scalar1=2.0, scalar2=0.0, op0=MULT, op1=ADD)

            vector_transpose(0, 0)
            regroup(l_grp[:], l_raw[:])
            quantise(0, 0)
            nc.vector.quantize_mx(
                out=l_codes[:].bitcast(E4X4), scales=l_scales[:], in_=l_grp[:].rearrange("p r t -> p (r t)")
            )
            make_t(0, 0, P)
            for i in range(2, 8):
                one_transpose(0, i)
            quantise(0, 1)
            quantise(0, 2)

            for i in range(S * H):
                first(0, i, low_pass)
                if i == 0:
                    make_t(0, P, CHUNK)
                ahead = 1 if i < 4 else 2
                one_transpose(ahead, 2 * (i % 4))
                one_transpose(ahead, 2 * (i % 4) + 1)
                if i == 2:
                    quantise(1, 0)
                if i == 4:
                    quantise(1, 1)
                    for h in range(H):
                        regroup(w_grp[:, h * HALF : (h + 1) * HALF, :], w_raw[:, :, h * HALF : (h + 1) * HALF])
                if i == 5:
                    quantise_w(0)
                    quantise_w(1)
                if i == 6:
                    make_t(1, 0, CHUNK)
                if i == 7:
                    quantise(2, 0)
            quantise(2, 1)

            for c in range(1, N_CHUNKS):
                for i in range(S * H):
                    if c == 1:
                        second(0, i, main_pass)
                    first(c, i, main_pass)
                    second(c, i, low_pass_any)
                    split(c, i)
                    if i == 2:
                        vector_transpose(c + 2, 0)
                    if i == 3:
                        make_t(c + 1, 0, CHUNK)
                    if i == 4:
                        vector_transpose(c + 2, 1)
                    if i == 6:
                        quantise(c + 2, 0)
                quantise(c + 2, 1)
